import numpy as np
import ml_dtypes


def mxq(x, axis, fmt="e4m3"):
    dtype, down = {"e4m3": (ml_dtypes.float8_e4m3fn, 7), "e5m2": (ml_dtypes.float8_e5m2, 14)}[fmt]
    v = np.moveaxis(np.asarray(x, np.float32).astype(ml_dtypes.bfloat16).astype(np.float64), axis, -1)
    blocks = v.reshape(v.shape[:-1] + (-1, 32))
    amax = np.abs(blocks).max(-1, keepdims=True)
    byte = np.maximum(np.where(amax > 0, np.frexp(amax)[1] - 1 + 127, 0) - down, 1)
    scale = np.exp2(byte - 127.0)
    codes = (blocks / scale).astype(np.float32).astype(dtype).astype(np.float64)
    return np.moveaxis((codes * scale).reshape(v.shape), -1, axis)


WIDE = False


def mx_kscale(k):
    if not WIDE:
        return np.ones(k)
    levels = np.array([10, -10, 5, -5, 0])
    a = np.random.permutation(np.resize(levels, k // 512 * 4)).reshape(k // 512, 4)
    idx = np.arange(k)
    return np.exp2(a[idx // 512, idx % 128 // 32])


BF16 = ml_dtypes.bfloat16


def bf(x):
    return np.asarray(x, np.float32).astype(BF16)


def f64(x):
    return np.asarray(x).astype(np.float64)


B, T, E, C, H, XB = 8, 1024, 512, 512, 4, 512
D = C // H
EPS = 1e-5


def silu(a):
    return a / (1.0 + np.exp(-a))


def setup_inputs():
    s, t = mx_kscale(E), mx_kscale(C)
    amp = 2.0 ** np.linspace(-8.0, 2.0, H)
    y = np.random.standard_normal((B, T, H, D)) * amp[None, None, :, None]
    return {"x": bf(np.random.standard_normal((B, T, E)) * s),
            "y_ret": bf(y.reshape(B, T, C)),
            "w_g": bf(np.random.standard_normal((E, C)) / np.sqrt(E) / s[:, None]),
            "w_proj": bf(np.random.standard_normal((C, E)) / np.sqrt(C) / t[:, None]),
            "gn_weight": bf((1.0 + 0.1 * np.random.standard_normal(C)) * t),
            "gn_bias": bf(0.1 * np.random.standard_normal(C) * t)}


def reference(x, y_ret, w_g, w_proj, gn_weight, gn_bias):
    yg = f64(y_ret).reshape(B * T, H, D)
    mu = yg.mean(axis=-1, keepdims=True)
    var = yg.var(axis=-1, keepdims=True)
    yn = (yg - mu) / np.sqrt(var + EPS)
    yn = yn.reshape(B * T, C) * f64(gn_weight)[None] + f64(gn_bias)[None]
    yn = yn.reshape(B, T, C)
    g = mxq(f64(x), 2, "e4m3") @ mxq(f64(w_g), 0, "e4m3")
    h = silu(g) * yn
    return mxq(h, 2, "e4m3") @ mxq(f64(w_proj), 0, "e4m3")

@@ -1,0 +1,175 @@
+from contextlib import ExitStack
+
+import concourse.mybir as mybir
+from concourse.masks import make_identity
+
+BF16 = mybir.dt.bfloat16
+F32 = mybir.dt.float32
+U32 = mybir.dt.uint32
+U8 = mybir.dt.uint8
+FP8X4 = mybir.dt.float8_e4m3fn_x4
+ACT = mybir.ActivationFunctionType
+ALU = mybir.AluOpType
+
+P = 128
+PACK = 4
+TOKENS = 8 * 1024
+WIDTH = 512
+HEADS = 4
+HEAD = WIDTH // HEADS
+TILES = 4
+BLOCK = TILES * P
+BLOCKS = TOKENS // BLOCK
+EPS = 1e-5
+
+FLOPS = 2 * 2 * TOKENS * WIDTH * WIDTH
+
+
+def tile_multiscaleretention_pc_t_kernel(tc, x, y_ret, w_g, w_proj, gn_weight, gn_bias, out):
+    nc = tc.nc
+    x_blocks = x.flatten_outer_dims().rearrange("(n p j) e -> n p j e", p=P, j=TILES)
+    y_blocks = y_ret.flatten_outer_dims().rearrange("(n p j) c -> n p j c", p=P, j=TILES)
+    out_blocks = out.flatten_outer_dims().rearrange("(n p j) e -> n p j e", p=P, j=TILES)
+
+    with ExitStack() as ctx:
+        consts = ctx.enter_context(tc.tile_pool(name="consts", bufs=1))
+        loads = ctx.enter_context(tc.tile_pool(name="loads", bufs=4))
+        work = ctx.enter_context(tc.tile_pool(name="work", bufs=3))
+        psum = ctx.enter_context(tc.psum_pool(name="psum", bufs=2))
+
+        def quantise(values, pool, name):
+            columns = values.shape[1] // PACK
+            codes = pool.tile([P, columns], U32, name=name + "_codes", align_bytes=64)
+            scales = pool.tile([P, columns], U8, name=name + "_scales", align_bytes=64)
+            nc.vector.quantize_mx(out=codes[:].bitcast(FP8X4), scales=scales[:], in_=values)
+            return codes, scales
+
+        def quantise_weight(rows, name):
+            raw = consts.tile([P, PACK, WIDTH], BF16, name=name + "_raw")
+            nc.sync.dma_start(out=raw[:], in_=rows)
+            grouped = consts.tile([P, WIDTH, PACK], BF16, name=name + "_grouped", align_bytes=64)
+            nc.vector.tensor_copy(out=grouped[:], in_=raw[:].rearrange("p t c -> p c t"))
+            return quantise(grouped[:].rearrange("p c t -> p (c t)"), consts, name)
+
+        ident_f32 = consts.tile([P, P], F32, name="ident_f32")
+        make_identity(nc, ident_f32[:])
+        ident_bf16 = consts.tile([P, P], BF16, name="ident_bf16")
+        make_identity(nc, ident_bf16[:])
+        minus_half = consts.tile([P, TILES * HEADS], F32, name="minus_half")
+        nc.vector.memset(minus_half[:], -0.5)
+
+        wg_raw = consts.tile([P, 2, 2, WIDTH], BF16, name="wg_raw")
+        nc.sync.dma_start(out=wg_raw[:], in_=w_g.rearrange("(u p e) c -> p u e c", u=2, e=2))
+        wg_grouped = consts.tile([P, WIDTH, PACK], BF16, name="wg_grouped", align_bytes=64)
+        nc.vector.tensor_copy(out=wg_grouped[:], in_=wg_raw[:].rearrange("p u e c -> p c (u e)"))
+        wg_codes, wg_scales = quantise(wg_grouped[:].rearrange("p c t -> p (c t)"), consts, "wg")
+        wp_codes, wp_scales = quantise_weight(w_proj.rearrange("(t p) n -> p t n", t=PACK), "wp")
+
+        affine_rows = consts.tile([P, P], BF16, name="affine_rows")
+        nc.vector.memset(affine_rows[:], 0.0)
+        nc.sync.dma_start(out=affine_rows[0:HEADS, :], in_=gn_weight.rearrange("(t p) -> t p", t=HEADS))
+        nc.sync.dma_start(out=affine_rows[HEADS : 2 * HEADS, :], in_=gn_bias.rearrange("(t p) -> t p", t=HEADS))
+        affine_ps = psum.tile([P, P], BF16, name="affine_ps", tag="xT")
+        nc.tensor.transpose(affine_ps[:], affine_rows[:], ident_bf16[:])
+        affine = consts.tile([P, 2 * HEADS], F32, name="affine")
+        nc.vector.tensor_copy(out=affine[:], in_=affine_ps[:, 0 : 2 * HEADS])
+
+        for n in range(BLOCKS):
+            x_sb = loads.tile([P, TILES, WIDTH], BF16, name="x_sb")
+            nc.sync.dma_start(out=x_sb[:], in_=x_blocks[n])
+            y_sb = loads.tile([P, TILES, WIDTH], BF16, name="y_sb")
+            nc.sync.dma_start(out=y_sb[:], in_=y_blocks[n])
+
+            stats = work.tile([P, TILES * HEADS, 3], F32, name="stats")
+            for j in range(TILES):
+                for h in range(0, HEADS, 2):
+                    nc.vector.bn_stats(
+                        out=stats[:, j * HEADS + h : j * HEADS + h + 2, :].rearrange("p h s -> p (h s)"),
+                        in_=y_sb[:, j, h * HEAD : (h + 2) * HEAD].rearrange("p (h c) -> p c h", h=2),
+                    )
+            var_eps = work.tile([P, TILES * HEADS], F32, name="var_eps")
+            nc.gpsimd.tensor_scalar(
+                out=var_eps[:], in0=stats[:, :, 2], scalar1=1.0 / HEAD, scalar2=EPS, op0=ALU.mult, op1=ALU.add
+            )
+            rstd = work.tile([P, TILES * HEADS], F32, name="rstd")
+            nc.gpsimd.tensor_tensor(out=rstd[:], in0=var_eps[:], in1=minus_half[:], op=ALU.pow)
+            z = work.tile([P, TILES, WIDTH], F32, name="z")
+            for j in range(TILES):
+                for h in range(HEADS):
+                    i = j * HEADS + h
+                    nc.vector.tensor_scalar(
+                        out=z[:, j, h * HEAD : (h + 1) * HEAD],
+                        in0=y_sb[:, j, h * HEAD : (h + 1) * HEAD],
+                        scalar1=stats[:, i, 1:2],
+                        scalar2=rstd[:, i : i + 1],
+                        op0=ALU.subtract,
+                        op1=ALU.mult,
+                    )
+
+            yn = work.tile([P, HEADS, BLOCK], F32, name="yn")
+            for h in range(HEADS):
+                zT = psum.tile([P, TILES, P], F32, name="zT")
+                for j in range(TILES):
+                    nc.tensor.transpose(zT[:, j, :], z[:, j, h * HEAD : (h + 1) * HEAD], ident_f32[:])
+                nc.scalar.activation(
+                    out=yn[:, h, :],
+                    in_=zT[:].rearrange("p j w -> p (j w)"),
+                    func=ACT.Identity,
+                    scale=affine[:, h : h + 1],
+                    bias=affine[:, HEADS + h : HEADS + h + 1],
+                )
+
+            x_grouped = work.tile([P, BLOCK * PACK], BF16, name="x_grouped", align_bytes=64)
+            x_words = x_grouped[:].bitcast(F32).rearrange("p (j w u) -> p j w u", j=TILES, u=2)
+            for half in range(TILES // 2):
+                xT = psum.tile([P, 2, 2, P], F32, name="xT")
+                for j in range(2):
+                    for u in range(2):
+                        nc.tensor.transpose(
+                            xT[:, j, u, :],
+                            x_sb[:, 2 * half + j, :].bitcast(F32)[:, u * P : (u + 1) * P],
+                            ident_f32[:],
+                        )
+                nc.scalar.copy(
+                    out=x_words[:, 2 * half : 2 * half + 2], in_=xT[:].rearrange("p j u w -> p j w u")
+                )
+            x_codes, x_scales = quantise(x_grouped[:], work, "x")
+
+            gate = work.tile([P, TILES, P, HEADS], F32, name="gate")
+            for j in range(TILES):
+                g_ps = psum.tile([P, HEADS, P], F32, name="g_ps")
+                for h in range(HEADS):
+                    nc.tensor.matmul_mx(
+                        out=g_ps[:, h, :],
+                        lhsT=wg_codes[:, h * HEAD : (h + 1) * HEAD].bitcast(FP8X4),
+                        lhsT_scale=wg_scales[:, h * HEAD : (h + 1) * HEAD],
+                        rhs=x_codes[:, j * P : (j + 1) * P].bitcast(FP8X4),
+                        rhs_scale=x_scales[:, j * P : (j + 1) * P],
+                        start=True,
+                        stop=True,
+                    )
+                nc.scalar.activation(out=gate[:, j], in_=g_ps[:].rearrange("p h w -> p w h"), func=ACT.Silu)
+
+            hidden = work.tile([P, BLOCK, PACK], BF16, name="hidden", align_bytes=64)
+            nc.vector.tensor_tensor(
+                out=hidden[:],
+                in0=gate[:].rearrange("p j w h -> p (j w) h"),
+                in1=yn[:].rearrange("p h n -> p n h"),
+                op=ALU.mult,
+            )
+            h_codes, h_scales = quantise(hidden[:].rearrange("p n h -> p (n h)"), work, "h")
+
+            out_sb = work.tile([P, TILES, WIDTH], F32, name="out_sb")
+            for j in range(TILES):
+                o_ps = psum.tile([P, WIDTH], F32, name="o_ps")
+                nc.tensor.matmul_mx(
+                    out=o_ps[:],
+                    lhsT=h_codes[:, j * P : (j + 1) * P].bitcast(FP8X4),
+                    lhsT_scale=h_scales[:, j * P : (j + 1) * P],
+                    rhs=wp_codes[:].bitcast(FP8X4),
+                    rhs_scale=wp_scales[:],
+                    start=True,
+                    stop=True,
+                )
+                nc.scalar.copy(out=out_sb[:, j, :], in_=o_ps[:])
+            nc.sync.dma_start(out=out_blocks[n], in_=out_sb[:])

@@ -21,6 +21,8 @@ TILES = 4
 BLOCK = TILES * P
 BLOCKS = TOKENS // BLOCK
 EPS = 1e-5
+LOAD_AHEAD = 3
+LAST_STAGE = 4
 
 FLOPS = 2 * 2 * TOKENS * WIDTH * WIDTH
 
@@ -32,10 +34,12 @@ def tile_multiscaleretention_pc_t_kernel(tc, x, y_ret, w_g, w_proj, gn_weight, g
     out_blocks = out.flatten_outer_dims().rearrange("(n p j) e -> n p j e", p=P, j=TILES)
 
     with ExitStack() as ctx:
+        ctx.enter_context(tc.manual_schedule())
         consts = ctx.enter_context(tc.tile_pool(name="consts", bufs=1))
-        loads = ctx.enter_context(tc.tile_pool(name="loads", bufs=4))
+        loads = ctx.enter_context(tc.tile_pool(name="loads", bufs=LOAD_AHEAD + 3))
         work = ctx.enter_context(tc.tile_pool(name="work", bufs=3))
-        psum = ctx.enter_context(tc.psum_pool(name="psum", bufs=2))
+        psum = ctx.enter_context(tc.psum_pool(name="psum", bufs=8))
+        live = {}
 
         def quantise(values, pool, name):
             columns = values.shape[1] // PACK
@@ -44,42 +48,16 @@ def tile_multiscaleretention_pc_t_kernel(tc, x, y_ret, w_g, w_proj, gn_weight, g
             nc.vector.quantize_mx(out=codes[:].bitcast(FP8X4), scales=scales[:], in_=values)
             return codes, scales
 
-        def quantise_weight(rows, name):
-            raw = consts.tile([P, PACK, WIDTH], BF16, name=name + "_raw")
-            nc.sync.dma_start(out=raw[:], in_=rows)
-            grouped = consts.tile([P, WIDTH, PACK], BF16, name=name + "_grouped", align_bytes=64)
-            nc.vector.tensor_copy(out=grouped[:], in_=raw[:].rearrange("p t c -> p c t"))
-            return quantise(grouped[:].rearrange("p c t -> p (c t)"), consts, name)
-
-        ident_f32 = consts.tile([P, P], F32, name="ident_f32")
-        make_identity(nc, ident_f32[:])
-        ident_bf16 = consts.tile([P, P], BF16, name="ident_bf16")
-        make_identity(nc, ident_bf16[:])
-        minus_half = consts.tile([P, TILES * HEADS], F32, name="minus_half")
-        nc.vector.memset(minus_half[:], -0.5)
-
-        wg_raw = consts.tile([P, 2, 2, WIDTH], BF16, name="wg_raw")
-        nc.sync.dma_start(out=wg_raw[:], in_=w_g.rearrange("(u p e) c -> p u e c", u=2, e=2))
-        wg_grouped = consts.tile([P, WIDTH, PACK], BF16, name="wg_grouped", align_bytes=64)
-        nc.vector.tensor_copy(out=wg_grouped[:], in_=wg_raw[:].rearrange("p u e c -> p c (u e)"))
-        wg_codes, wg_scales = quantise(wg_grouped[:].rearrange("p c t -> p (c t)"), consts, "wg")
-        wp_codes, wp_scales = quantise_weight(w_proj.rearrange("(t p) n -> p t n", t=PACK), "wp")
-
-        affine_rows = consts.tile([P, P], BF16, name="affine_rows")
-        nc.vector.memset(affine_rows[:], 0.0)
-        nc.sync.dma_start(out=affine_rows[0:HEADS, :], in_=gn_weight.rearrange("(t p) -> t p", t=HEADS))
-        nc.sync.dma_start(out=affine_rows[HEADS : 2 * HEADS, :], in_=gn_bias.rearrange("(t p) -> t p", t=HEADS))
-        affine_ps = psum.tile([P, P], BF16, name="affine_ps", tag="xT")
-        nc.tensor.transpose(affine_ps[:], affine_rows[:], ident_bf16[:])
-        affine = consts.tile([P, 2 * HEADS], F32, name="affine")
-        nc.vector.tensor_copy(out=affine[:], in_=affine_ps[:, 0 : 2 * HEADS])
-
-        for n in range(BLOCKS):
+        def load(n):
             x_sb = loads.tile([P, TILES, WIDTH], BF16, name="x_sb")
             nc.sync.dma_start(out=x_sb[:], in_=x_blocks[n])
             y_sb = loads.tile([P, TILES, WIDTH], BF16, name="y_sb")
             nc.sync.dma_start(out=y_sb[:], in_=y_blocks[n])
+            live["x_sb", n] = x_sb
+            live["y_sb", n] = y_sb
 
+        def statistics(n):
+            y_sb = live["y_sb", n]
             stats = work.tile([P, TILES * HEADS, 3], F32, name="stats")
             for j in range(TILES):
                 for h in range(0, HEADS, 2):
@@ -93,6 +71,11 @@ def tile_multiscaleretention_pc_t_kernel(tc, x, y_ret, w_g, w_proj, gn_weight, g
             )
             rstd = work.tile([P, TILES * HEADS], F32, name="rstd")
             nc.gpsimd.tensor_tensor(out=rstd[:], in0=var_eps[:], in1=minus_half[:], op=ALU.pow)
+            live["stats", n] = stats
+            live["rstd", n] = rstd
+
+        def centre_and_scale(n):
+            y_sb, stats, rstd = live["y_sb", n], live["stats", n], live["rstd", n]
             z = work.tile([P, TILES, WIDTH], F32, name="z")
             for j in range(TILES):
                 for h in range(HEADS):
@@ -105,24 +88,30 @@ def tile_multiscaleretention_pc_t_kernel(tc, x, y_ret, w_g, w_proj, gn_weight, g
                         op0=ALU.subtract,
                         op1=ALU.mult,
                     )
+            live["z", n] = z
 
+        def affine(n):
+            z = live["z", n]
             yn = work.tile([P, HEADS, BLOCK], F32, name="yn")
             for h in range(HEADS):
-                zT = psum.tile([P, TILES, P], F32, name="zT")
+                zT = psum.tile([P, TILES, P], F32, name="zT", tag="bank")
                 for j in range(TILES):
                     nc.tensor.transpose(zT[:, j, :], z[:, j, h * HEAD : (h + 1) * HEAD], ident_f32[:])
                 nc.scalar.activation(
                     out=yn[:, h, :],
                     in_=zT[:].rearrange("p j w -> p (j w)"),
                     func=ACT.Identity,
-                    scale=affine[:, h : h + 1],
-                    bias=affine[:, HEADS + h : HEADS + h + 1],
+                    scale=gain_bias[:, h : h + 1],
+                    bias=gain_bias[:, HEADS + h : HEADS + h + 1],
                 )
+            live["yn", n] = yn
 
+        def transpose_tokens(n):
+            x_sb = live["x_sb", n]
             x_grouped = work.tile([P, BLOCK * PACK], BF16, name="x_grouped", align_bytes=64)
             x_words = x_grouped[:].bitcast(F32).rearrange("p (j w u) -> p j w u", j=TILES, u=2)
             for half in range(TILES // 2):
-                xT = psum.tile([P, 2, 2, P], F32, name="xT")
+                xT = psum.tile([P, 2, 2, P], F32, name="xT", tag="bank")
                 for j in range(2):
                     for u in range(2):
                         nc.tensor.transpose(
@@ -133,11 +122,16 @@ def tile_multiscaleretention_pc_t_kernel(tc, x, y_ret, w_g, w_proj, gn_weight, g
                 nc.scalar.copy(
                     out=x_words[:, 2 * half : 2 * half + 2], in_=xT[:].rearrange("p j u w -> p j w u")
                 )
-            x_codes, x_scales = quantise(x_grouped[:], work, "x")
+            live["x_grouped", n] = x_grouped
 
-            gate = work.tile([P, TILES, P, HEADS], F32, name="gate")
+        def quantise_tokens(n):
+            live["x_mx", n] = quantise(live["x_grouped", n][:], work, "x")
+
+        def gate(n):
+            x_codes, x_scales = live["x_mx", n]
+            gated = work.tile([P, TILES, P, HEADS], F32, name="gated")
             for j in range(TILES):
-                g_ps = psum.tile([P, HEADS, P], F32, name="g_ps")
+                g_ps = psum.tile([P, HEADS, P], F32, name="g_ps", tag="bank")
                 for h in range(HEADS):
                     nc.tensor.matmul_mx(
                         out=g_ps[:, h, :],
@@ -148,20 +142,27 @@ def tile_multiscaleretention_pc_t_kernel(tc, x, y_ret, w_g, w_proj, gn_weight, g
                         start=True,
                         stop=True,
                     )
-                nc.scalar.activation(out=gate[:, j], in_=g_ps[:].rearrange("p h w -> p w h"), func=ACT.Silu)
+                nc.scalar.activation(out=gated[:, j], in_=g_ps[:].rearrange("p h w -> p w h"), func=ACT.Silu)
+            live["gated", n] = gated
 
+        def multiply(n):
             hidden = work.tile([P, BLOCK, PACK], BF16, name="hidden", align_bytes=64)
             nc.vector.tensor_tensor(
                 out=hidden[:],
-                in0=gate[:].rearrange("p j w h -> p (j w) h"),
-                in1=yn[:].rearrange("p h n -> p n h"),
+                in0=live["gated", n][:].rearrange("p j w h -> p (j w) h"),
+                in1=live["yn", n][:].rearrange("p h n -> p n h"),
                 op=ALU.mult,
             )
-            h_codes, h_scales = quantise(hidden[:].rearrange("p n h -> p (n h)"), work, "h")
+            live["hidden", n] = hidden
 
+        def quantise_hidden(n):
+            live["h_mx", n] = quantise(live["hidden", n][:].rearrange("p n h -> p (n h)"), work, "h")
+
+        def project(n):
+            h_codes, h_scales = live["h_mx", n]
             out_sb = work.tile([P, TILES, WIDTH], F32, name="out_sb")
             for j in range(TILES):
-                o_ps = psum.tile([P, WIDTH], F32, name="o_ps")
+                o_ps = psum.tile([P, WIDTH], F32, name="o_ps", tag="bank")
                 nc.tensor.matmul_mx(
                     out=o_ps[:],
                     lhsT=h_codes[:, j * P : (j + 1) * P].bitcast(FP8X4),
@@ -173,3 +174,54 @@ def tile_multiscaleretention_pc_t_kernel(tc, x, y_ret, w_g, w_proj, gn_weight, g
                 )
                 nc.scalar.copy(out=out_sb[:, j, :], in_=o_ps[:])
             nc.sync.dma_start(out=out_blocks[n], in_=out_sb[:])
+
+        load(0)
+        wg_raw = consts.tile([P, PACK, WIDTH], BF16, name="wg_raw")
+        nc.sync.dma_start(
+            out=wg_raw[:].rearrange("p (u e) c -> p u e c", u=2), in_=w_g.rearrange("(u p e) c -> p u e c", u=2, e=2)
+        )
+        affine_rows = consts.tile([P, P], BF16, name="affine_rows")
+        nc.vector.memset(affine_rows[:], 0.0)
+        nc.sync.dma_start(out=affine_rows[0:HEADS, :], in_=gn_weight.rearrange("(t p) -> t p", t=HEADS))
+        nc.sync.dma_start(out=affine_rows[HEADS : 2 * HEADS, :], in_=gn_bias.rearrange("(t p) -> t p", t=HEADS))
+        wp_raw = consts.tile([P, PACK, WIDTH], BF16, name="wp_raw")
+        nc.sync.dma_start(out=wp_raw[:], in_=w_proj.rearrange("(t p) n -> p t n", t=PACK))
+        for n in range(1, LOAD_AHEAD):
+            load(n)
+
+        ident_f32 = consts.tile([P, P], F32, name="ident_f32")
+        make_identity(nc, ident_f32[:])
+        ident_bf16 = consts.tile([P, P], BF16, name="ident_bf16")
+        make_identity(nc, ident_bf16[:])
+        minus_half = consts.tile([P, TILES * HEADS], F32, name="minus_half")
+        nc.vector.memset(minus_half[:], -0.5)
+        table_warmer = consts.tile([P, 1], F32, name="table_warmer")
+        nc.scalar.activation(out=table_warmer[:], in_=minus_half[:, 0:1], func=ACT.Silu)
+
+        wg_grouped = consts.tile([P, WIDTH, PACK], BF16, name="wg_grouped", align_bytes=64)
+        nc.vector.tensor_copy(out=wg_grouped[:], in_=wg_raw[:].rearrange("p t c -> p c t"))
+        wp_grouped = consts.tile([P, WIDTH, PACK], BF16, name="wp_grouped", align_bytes=64)
+        nc.vector.tensor_copy(out=wp_grouped[:], in_=wp_raw[:].rearrange("p t c -> p c t"))
+        wg_codes, wg_scales = quantise(wg_grouped[:].rearrange("p c t -> p (c t)"), consts, "wg")
+        wp_codes, wp_scales = quantise(wp_grouped[:].rearrange("p c t -> p (c t)"), consts, "wp")
+
+        affine_ps = psum.tile([P, P], BF16, name="affine_ps", tag="bank")
+        nc.tensor.transpose(affine_ps[:], affine_rows[:], ident_bf16[:])
+        gain_bias = consts.tile([P, 2 * HEADS], F32, name="gain_bias")
+        nc.vector.tensor_copy(out=gain_bias[:], in_=affine_ps[:, 0 : 2 * HEADS])
+
+        def run(stage, n):
+            if 0 <= n < BLOCKS:
+                stage(n)
+
+        for step in range(BLOCKS + LAST_STAGE):
+            run(statistics, step)
+            run(multiply, step - 3)
+            run(quantise_tokens, step - 1)
+            run(quantise_hidden, step - 3)
+            run(centre_and_scale, step - 1)
+            run(transpose_tokens, step)
+            run(affine, step - 2)
+            run(gate, step - 2)
+            run(project, step - 4)
+            run(load, step + LOAD_AHEAD)

@@ -23,6 +23,8 @@ BLOCKS = TOKENS // BLOCK
 EPS = 1e-5
 LOAD_AHEAD = 3
 LAST_STAGE = 4
+WEIGHTS_STEP = 1
+GPSIMD_TILES = 2
 
 FLOPS = 2 * 2 * TOKENS * WIDTH * WIDTH
 
@@ -129,6 +131,7 @@ def tile_multiscaleretention_pc_t_kernel(tc, x, y_ret, w_g, w_proj, gn_weight, g
 
         def gate(n):
             x_codes, x_scales = live["x_mx", n]
+            wg_codes, wg_scales = live["wg_mx"]
             gated = work.tile([P, TILES, P, HEADS], F32, name="gated")
             for j in range(TILES):
                 g_ps = psum.tile([P, HEADS, P], F32, name="g_ps", tag="bank")
@@ -145,21 +148,28 @@ def tile_multiscaleretention_pc_t_kernel(tc, x, y_ret, w_g, w_proj, gn_weight, g
                 nc.scalar.activation(out=gated[:, j], in_=g_ps[:].rearrange("p h w -> p w h"), func=ACT.Silu)
             live["gated", n] = gated
 
-        def multiply(n):
-            hidden = work.tile([P, BLOCK, PACK], BF16, name="hidden", align_bytes=64)
-            nc.vector.tensor_tensor(
-                out=hidden[:],
-                in0=live["gated", n][:].rearrange("p j w h -> p (j w) h"),
-                in1=live["yn", n][:].rearrange("p h n -> p n h"),
+        def multiply(engine, n, first, last):
+            engine.tensor_tensor(
+                out=live["hidden", n][:, first * P : last * P, :],
+                in0=live["gated", n][:, first:last].rearrange("p j w h -> p (j w) h"),
+                in1=live["yn", n][:, :, first * P : last * P].rearrange("p h n -> p n h"),
                 op=ALU.mult,
             )
+
+        def multiply_on_gpsimd(n):
+            hidden = work.tile([P, BLOCK, PACK], BF16, name="hidden", align_bytes=64)
             live["hidden", n] = hidden
+            multiply(nc.gpsimd, n, 0, GPSIMD_TILES)
+
+        def multiply_on_vector(n):
+            multiply(nc.vector, n, GPSIMD_TILES, TILES)
 
         def quantise_hidden(n):
             live["h_mx", n] = quantise(live["hidden", n][:].rearrange("p n h -> p (n h)"), work, "h")
 
         def project(n):
             h_codes, h_scales = live["h_mx", n]
+            wp_codes, wp_scales = live["wp_mx"]
             out_sb = work.tile([P, TILES, WIDTH], F32, name="out_sb")
             for j in range(TILES):
                 o_ps = psum.tile([P, WIDTH], F32, name="o_ps", tag="bank")
@@ -172,8 +182,23 @@ def tile_multiscaleretention_pc_t_kernel(tc, x, y_ret, w_g, w_proj, gn_weight, g
                     start=True,
                     stop=True,
                 )
-                nc.scalar.copy(out=out_sb[:, j, :], in_=o_ps[:])
-            nc.sync.dma_start(out=out_blocks[n], in_=out_sb[:])
+                if j < GPSIMD_TILES:
+                    nc.vector.tensor_copy(out=out_sb[:, j, :], in_=o_ps[:])
+                else:
+                    nc.scalar.copy(out=out_sb[:, j, :], in_=o_ps[:])
+            nc.sync.dma_start(out=out_blocks[n][:, 0:GPSIMD_TILES, :], in_=out_sb[:, 0:GPSIMD_TILES, :])
+            nc.sync.dma_start(out=out_blocks[n][:, GPSIMD_TILES:TILES, :], in_=out_sb[:, GPSIMD_TILES:TILES, :])
+
+        def prepare_weights():
+            wg_grouped = consts.tile([P, WIDTH, PACK], BF16, name="wg_grouped", align_bytes=64)
+            nc.vector.tensor_copy(out=wg_grouped[:], in_=wg_raw[:].rearrange("p t c -> p c t"))
+            wp_grouped = consts.tile([P, WIDTH, PACK], BF16, name="wp_grouped", align_bytes=64)
+            nc.vector.tensor_copy(out=wp_grouped[:], in_=wp_raw[:].rearrange("p t c -> p c t"))
+            live["wg_mx"] = quantise(wg_grouped[:].rearrange("p c t -> p (c t)"), consts, "wg")
+            live["wp_mx"] = quantise(wp_grouped[:].rearrange("p c t -> p (c t)"), consts, "wp")
+            affine_ps = psum.tile([P, P], BF16, name="affine_ps", tag="bank")
+            nc.tensor.transpose(affine_ps[:], affine_rows[:], ident_bf16[:])
+            nc.vector.tensor_copy(out=gain_bias[:], in_=affine_ps[:, 0 : 2 * HEADS])
 
         load(0)
         wg_raw = consts.tile([P, PACK, WIDTH], BF16, name="wg_raw")
@@ -195,33 +220,25 @@ def tile_multiscaleretention_pc_t_kernel(tc, x, y_ret, w_g, w_proj, gn_weight, g
         make_identity(nc, ident_bf16[:])
         minus_half = consts.tile([P, TILES * HEADS], F32, name="minus_half")
         nc.vector.memset(minus_half[:], -0.5)
+        gain_bias = consts.tile([P, 2 * HEADS], F32, name="gain_bias")
         table_warmer = consts.tile([P, 1], F32, name="table_warmer")
         nc.scalar.activation(out=table_warmer[:], in_=minus_half[:, 0:1], func=ACT.Silu)
-
-        wg_grouped = consts.tile([P, WIDTH, PACK], BF16, name="wg_grouped", align_bytes=64)
-        nc.vector.tensor_copy(out=wg_grouped[:], in_=wg_raw[:].rearrange("p t c -> p c t"))
-        wp_grouped = consts.tile([P, WIDTH, PACK], BF16, name="wp_grouped", align_bytes=64)
-        nc.vector.tensor_copy(out=wp_grouped[:], in_=wp_raw[:].rearrange("p t c -> p c t"))
-        wg_codes, wg_scales = quantise(wg_grouped[:].rearrange("p c t -> p (c t)"), consts, "wg")
-        wp_codes, wp_scales = quantise(wp_grouped[:].rearrange("p c t -> p (c t)"), consts, "wp")
-
-        affine_ps = psum.tile([P, P], BF16, name="affine_ps", tag="bank")
-        nc.tensor.transpose(affine_ps[:], affine_rows[:], ident_bf16[:])
-        gain_bias = consts.tile([P, 2 * HEADS], F32, name="gain_bias")
-        nc.vector.tensor_copy(out=gain_bias[:], in_=affine_ps[:, 0 : 2 * HEADS])
 
         def run(stage, n):
             if 0 <= n < BLOCKS:
                 stage(n)
 
         for step in range(BLOCKS + LAST_STAGE):
+            if step == WEIGHTS_STEP:
+                prepare_weights()
+            run(multiply_on_gpsimd, step - 3)
             run(statistics, step)
-            run(multiply, step - 3)
+            run(project, step - 4)
+            run(multiply_on_vector, step - 3)
             run(quantise_tokens, step - 1)
             run(quantise_hidden, step - 3)
             run(centre_and_scale, step - 1)
-            run(transpose_tokens, step)
-            run(affine, step - 2)
             run(gate, step - 2)
-            run(project, step - 4)
+            run(affine, step - 2)
+            run(transpose_tokens, step)
             run(load, step + LOAD_AHEAD)

@@ -24,7 +24,7 @@ EPS = 1e-5
 LOAD_AHEAD = 3
 LAST_STAGE = 4
 WEIGHTS_STEP = 1
-GPSIMD_TILES = 2
+VECTOR_BANKS = 1
 
 FLOPS = 2 * 2 * TOKENS * WIDTH * WIDTH
 
@@ -51,10 +51,10 @@ def tile_multiscaleretention_pc_t_kernel(tc, x, y_ret, w_g, w_proj, gn_weight, g
             return codes, scales
 
         def load(n):
-            x_sb = loads.tile([P, TILES, WIDTH], BF16, name="x_sb")
-            nc.sync.dma_start(out=x_sb[:], in_=x_blocks[n])
             y_sb = loads.tile([P, TILES, WIDTH], BF16, name="y_sb")
             nc.sync.dma_start(out=y_sb[:], in_=y_blocks[n])
+            x_sb = loads.tile([P, TILES, WIDTH], BF16, name="x_sb")
+            nc.sync.dma_start(out=x_sb[:], in_=x_blocks[n])
             live["x_sb", n] = x_sb
             live["y_sb", n] = y_sb
 
@@ -148,21 +148,15 @@ def tile_multiscaleretention_pc_t_kernel(tc, x, y_ret, w_g, w_proj, gn_weight, g
                 nc.scalar.activation(out=gated[:, j], in_=g_ps[:].rearrange("p h w -> p w h"), func=ACT.Silu)
             live["gated", n] = gated
 
-        def multiply(engine, n, first, last):
-            engine.tensor_tensor(
-                out=live["hidden", n][:, first * P : last * P, :],
-                in0=live["gated", n][:, first:last].rearrange("p j w h -> p (j w) h"),
-                in1=live["yn", n][:, :, first * P : last * P].rearrange("p h n -> p n h"),
+        def multiply(n):
+            hidden = work.tile([P, BLOCK, PACK], BF16, name="hidden", align_bytes=64)
+            nc.vector.tensor_tensor(
+                out=hidden[:],
+                in0=live["gated", n][:].rearrange("p j w h -> p (j w) h"),
+                in1=live["yn", n][:].rearrange("p h n -> p n h"),
                 op=ALU.mult,
             )
-
-        def multiply_on_gpsimd(n):
-            hidden = work.tile([P, BLOCK, PACK], BF16, name="hidden", align_bytes=64)
             live["hidden", n] = hidden
-            multiply(nc.gpsimd, n, 0, GPSIMD_TILES)
-
-        def multiply_on_vector(n):
-            multiply(nc.vector, n, GPSIMD_TILES, TILES)
 
         def quantise_hidden(n):
             live["h_mx", n] = quantise(live["hidden", n][:].rearrange("p n h -> p (n h)"), work, "h")
@@ -182,12 +176,11 @@ def tile_multiscaleretention_pc_t_kernel(tc, x, y_ret, w_g, w_proj, gn_weight, g
                     start=True,
                     stop=True,
                 )
-                if j < GPSIMD_TILES:
+                if j < VECTOR_BANKS:
                     nc.vector.tensor_copy(out=out_sb[:, j, :], in_=o_ps[:])
                 else:
                     nc.scalar.copy(out=out_sb[:, j, :], in_=o_ps[:])
-            nc.sync.dma_start(out=out_blocks[n][:, 0:GPSIMD_TILES, :], in_=out_sb[:, 0:GPSIMD_TILES, :])
-            nc.sync.dma_start(out=out_blocks[n][:, GPSIMD_TILES:TILES, :], in_=out_sb[:, GPSIMD_TILES:TILES, :])
+                nc.sync.dma_start(out=out_blocks[n][:, j, :], in_=out_sb[:, j, :])
 
         def prepare_weights():
             wg_grouped = consts.tile([P, WIDTH, PACK], BF16, name="wg_grouped", align_bytes=64)
@@ -229,14 +222,13 @@ def tile_multiscaleretention_pc_t_kernel(tc, x, y_ret, w_g, w_proj, gn_weight, g
                 stage(n)
 
         for step in range(BLOCKS + LAST_STAGE):
+            run(quantise_tokens, step - 1)
             if step == WEIGHTS_STEP:
                 prepare_weights()
-            run(multiply_on_gpsimd, step - 3)
-            run(statistics, step)
+            run(multiply, step - 3)
             run(project, step - 4)
-            run(multiply_on_vector, step - 3)
-            run(quantise_tokens, step - 1)
             run(quantise_hidden, step - 3)
+            run(statistics, step)
             run(centre_and_scale, step - 1)
             run(gate, step - 2)
             run(affine, step - 2)

@@ -24,7 +24,8 @@ EPS = 1e-5
 LOAD_AHEAD = 3
 LAST_STAGE = 4
 WEIGHTS_STEP = 1
-VECTOR_BANKS = 1
+VECTOR_BANKS = 0
+RUN = 4
 
 FLOPS = 2 * 2 * TOKENS * WIDTH * WIDTH
 
@@ -132,7 +133,7 @@ def tile_multiscaleretention_pc_t_kernel(tc, x, y_ret, w_g, w_proj, gn_weight, g
         def gate(n):
             x_codes, x_scales = live["x_mx", n]
             wg_codes, wg_scales = live["wg_mx"]
-            gated = work.tile([P, TILES, P, HEADS], F32, name="gated")
+            gated = work.tile([P, TILES, P // RUN, HEADS, RUN], F32, name="gated")
             for j in range(TILES):
                 g_ps = psum.tile([P, HEADS, P], F32, name="g_ps", tag="bank")
                 for h in range(HEADS):
@@ -145,15 +146,17 @@ def tile_multiscaleretention_pc_t_kernel(tc, x, y_ret, w_g, w_proj, gn_weight, g
                         start=True,
                         stop=True,
                     )
-                nc.scalar.activation(out=gated[:, j], in_=g_ps[:].rearrange("p h w -> p w h"), func=ACT.Silu)
+                nc.scalar.activation(
+                    out=gated[:, j], in_=g_ps[:].rearrange("p h (c i) -> p c h i", i=RUN), func=ACT.Silu
+                )
             live["gated", n] = gated
 
         def multiply(n):
             hidden = work.tile([P, BLOCK, PACK], BF16, name="hidden", align_bytes=64)
             nc.vector.tensor_tensor(
-                out=hidden[:],
-                in0=live["gated", n][:].rearrange("p j w h -> p (j w) h"),
-                in1=live["yn", n][:].rearrange("p h n -> p n h"),
+                out=hidden[:].rearrange("p (c i) h -> p c h i", i=RUN),
+                in0=live["gated", n][:].rearrange("p j c h i -> p (j c) h i"),
+                in1=live["yn", n][:].rearrange("p h (c i) -> p c h i", i=RUN),
                 op=ALU.mult,
             )
             live["hidden", n] = hidden

@@ -25,6 +25,7 @@ LOAD_AHEAD = 3
 LAST_STAGE = 4
 WEIGHTS_STEP = 1
 VECTOR_BANKS = 0
+GPSIMD_TILES = 1
 RUN = 4
 
 FLOPS = 2 * 2 * TOKENS * WIDTH * WIDTH
@@ -153,12 +154,13 @@ def tile_multiscaleretention_pc_t_kernel(tc, x, y_ret, w_g, w_proj, gn_weight, g
 
         def multiply(n):
             hidden = work.tile([P, BLOCK, PACK], BF16, name="hidden", align_bytes=64)
-            nc.vector.tensor_tensor(
-                out=hidden[:].rearrange("p (c i) h -> p c h i", i=RUN),
-                in0=live["gated", n][:].rearrange("p j c h i -> p (j c) h i"),
-                in1=live["yn", n][:].rearrange("p h (c i) -> p c h i", i=RUN),
-                op=ALU.mult,
-            )
+            for engine, first, last in ((nc.gpsimd, 0, GPSIMD_TILES), (nc.vector, GPSIMD_TILES, TILES)):
+                engine.tensor_tensor(
+                    out=hidden[:, first * P : last * P, :].rearrange("p (c i) h -> p c h i", i=RUN),
+                    in0=live["gated", n][:, first:last].rearrange("p j c h i -> p (j c) h i"),
+                    in1=live["yn", n][:, :, first * P : last * P].rearrange("p h (c i) -> p c h i", i=RUN),
+                    op=ALU.mult,
+                )
             live["hidden", n] = hidden
 
         def quantise_hidden(n):
@@ -229,10 +231,10 @@ def tile_multiscaleretention_pc_t_kernel(tc, x, y_ret, w_g, w_proj, gn_weight, g
             if step == WEIGHTS_STEP:
                 prepare_weights()
             run(multiply, step - 3)
-            run(project, step - 4)
-            run(quantise_hidden, step - 3)
             run(statistics, step)
+            run(quantise_hidden, step - 3)
             run(centre_and_scale, step - 1)
+            run(project, step - 4)
             run(gate, step - 2)
             run(affine, step - 2)
             run(transpose_tokens, step)

from contextlib import ExitStack

import concourse.mybir as mybir
from concourse.masks import make_identity

BF16 = mybir.dt.bfloat16
F32 = mybir.dt.float32
U32 = mybir.dt.uint32
U8 = mybir.dt.uint8
FP8X4 = mybir.dt.float8_e4m3fn_x4
ACT = mybir.ActivationFunctionType
ALU = mybir.AluOpType

P = 128
PACK = 4
TOKENS = 8 * 1024
WIDTH = 512
HEADS = 4
HEAD = WIDTH // HEADS
TILES = 4
BLOCK = TILES * P
BLOCKS = TOKENS // BLOCK
EPS = 1e-5
LOAD_AHEAD = 3
LAST_STAGE = 4
WEIGHTS_STEP = 1
VECTOR_BANKS = 0
GPSIMD_TILES = 1
RUN = 4

FLOPS = 2 * 2 * TOKENS * WIDTH * WIDTH


def tile_multiscaleretention_pc_t_kernel(tc, x, y_ret, w_g, w_proj, gn_weight, gn_bias, out):
    nc = tc.nc
    x_blocks = x.flatten_outer_dims().rearrange("(n p j) e -> n p j e", p=P, j=TILES)
    y_blocks = y_ret.flatten_outer_dims().rearrange("(n p j) c -> n p j c", p=P, j=TILES)
    out_blocks = out.flatten_outer_dims().rearrange("(n p j) e -> n p j e", p=P, j=TILES)

    with ExitStack() as ctx:
        ctx.enter_context(tc.manual_schedule())
        consts = ctx.enter_context(tc.tile_pool(name="consts", bufs=1))
        loads = ctx.enter_context(tc.tile_pool(name="loads", bufs=LOAD_AHEAD + 3))
        work = ctx.enter_context(tc.tile_pool(name="work", bufs=3))
        psum = ctx.enter_context(tc.psum_pool(name="psum", bufs=8))
        live = {}

        def quantise(values, pool, name):
            columns = values.shape[1] // PACK
            codes = pool.tile([P, columns], U32, name=name + "_codes", align_bytes=64)
            scales = pool.tile([P, columns], U8, name=name + "_scales", align_bytes=64)
            nc.vector.quantize_mx(out=codes[:].bitcast(FP8X4), scales=scales[:], in_=values)
            return codes, scales

        def load(n):
            y_sb = loads.tile([P, TILES, WIDTH], BF16, name="y_sb")
            nc.sync.dma_start(out=y_sb[:], in_=y_blocks[n])
            x_sb = loads.tile([P, TILES, WIDTH], BF16, name="x_sb")
            nc.sync.dma_start(out=x_sb[:], in_=x_blocks[n])
            live["x_sb", n] = x_sb
            live["y_sb", n] = y_sb

        def statistics(n):
            y_sb = live["y_sb", n]
            stats = work.tile([P, TILES * HEADS, 3], F32, name="stats")
            for j in range(TILES):
                for h in range(0, HEADS, 2):
                    nc.vector.bn_stats(
                        out=stats[:, j * HEADS + h : j * HEADS + h + 2, :].rearrange("p h s -> p (h s)"),
                        in_=y_sb[:, j, h * HEAD : (h + 2) * HEAD].rearrange("p (h c) -> p c h", h=2),
                    )
            var_eps = work.tile([P, TILES * HEADS], F32, name="var_eps")
            nc.gpsimd.tensor_scalar(
                out=var_eps[:], in0=stats[:, :, 2], scalar1=1.0 / HEAD, scalar2=EPS, op0=ALU.mult, op1=ALU.add
            )
            rstd = work.tile([P, TILES * HEADS], F32, name="rstd")
            nc.gpsimd.tensor_tensor(out=rstd[:], in0=var_eps[:], in1=minus_half[:], op=ALU.pow)
            live["stats", n] = stats
            live["rstd", n] = rstd

        def centre_and_scale(n):
            y_sb, stats, rstd = live["y_sb", n], live["stats", n], live["rstd", n]
            z = work.tile([P, TILES, WIDTH], F32, name="z")
            for j in range(TILES):
                for h in range(HEADS):
                    i = j * HEADS + h
                    nc.vector.tensor_scalar(
                        out=z[:, j, h * HEAD : (h + 1) * HEAD],
                        in0=y_sb[:, j, h * HEAD : (h + 1) * HEAD],
                        scalar1=stats[:, i, 1:2],
                        scalar2=rstd[:, i : i + 1],
                        op0=ALU.subtract,
                        op1=ALU.mult,
                    )
            live["z", n] = z

        def affine(n):
            z = live["z", n]
            yn = work.tile([P, HEADS, BLOCK], F32, name="yn")
            for h in range(HEADS):
                zT = psum.tile([P, TILES, P], F32, name="zT", tag="bank")
                for j in range(TILES):
                    nc.tensor.transpose(zT[:, j, :], z[:, j, h * HEAD : (h + 1) * HEAD], ident_f32[:])
                nc.scalar.activation(
                    out=yn[:, h, :],
                    in_=zT[:].rearrange("p j w -> p (j w)"),
                    func=ACT.Identity,
                    scale=gain_bias[:, h : h + 1],
                    bias=gain_bias[:, HEADS + h : HEADS + h + 1],
                )
            live["yn", n] = yn

        def transpose_tokens(n):
            x_sb = live["x_sb", n]
            x_grouped = work.tile([P, BLOCK * PACK], BF16, name="x_grouped", align_bytes=64)
            x_words = x_grouped[:].bitcast(F32).rearrange("p (j w u) -> p j w u", j=TILES, u=2)
            for half in range(TILES // 2):
                xT = psum.tile([P, 2, 2, P], F32, name="xT", tag="bank")
                for j in range(2):
                    for u in range(2):
                        nc.tensor.transpose(
                            xT[:, j, u, :],
                            x_sb[:, 2 * half + j, :].bitcast(F32)[:, u * P : (u + 1) * P],
                            ident_f32[:],
                        )
                nc.scalar.copy(
                    out=x_words[:, 2 * half : 2 * half + 2], in_=xT[:].rearrange("p j u w -> p j w u")
                )
            live["x_grouped", n] = x_grouped

        def quantise_tokens(n):
            live["x_mx", n] = quantise(live["x_grouped", n][:], work, "x")

        def gate(n):
            x_codes, x_scales = live["x_mx", n]
            wg_codes, wg_scales = live["wg_mx"]
            gated = work.tile([P, TILES, P // RUN, HEADS, RUN], F32, name="gated")
            for j in range(TILES):
                g_ps = psum.tile([P, HEADS, P], F32, name="g_ps", tag="bank")
                for h in range(HEADS):
                    nc.tensor.matmul_mx(
                        out=g_ps[:, h, :],
                        lhsT=wg_codes[:, h * HEAD : (h + 1) * HEAD].bitcast(FP8X4),
                        lhsT_scale=wg_scales[:, h * HEAD : (h + 1) * HEAD],
                        rhs=x_codes[:, j * P : (j + 1) * P].bitcast(FP8X4),
                        rhs_scale=x_scales[:, j * P : (j + 1) * P],
                        start=True,
                        stop=True,
                    )
                nc.scalar.activation(
                    out=gated[:, j], in_=g_ps[:].rearrange("p h (c i) -> p c h i", i=RUN), func=ACT.Silu
                )
            live["gated", n] = gated

        def multiply(n):
            hidden = work.tile([P, BLOCK, PACK], BF16, name="hidden", align_bytes=64)
            for engine, first, last in ((nc.gpsimd, 0, GPSIMD_TILES), (nc.vector, GPSIMD_TILES, TILES)):
                engine.tensor_tensor(
                    out=hidden[:, first * P : last * P, :].rearrange("p (c i) h -> p c h i", i=RUN),
                    in0=live["gated", n][:, first:last].rearrange("p j c h i -> p (j c) h i"),
                    in1=live["yn", n][:, :, first * P : last * P].rearrange("p h (c i) -> p c h i", i=RUN),
                    op=ALU.mult,
                )
            live["hidden", n] = hidden

        def quantise_hidden(n):
            live["h_mx", n] = quantise(live["hidden", n][:].rearrange("p n h -> p (n h)"), work, "h")

        def project(n):
            h_codes, h_scales = live["h_mx", n]
            wp_codes, wp_scales = live["wp_mx"]
            out_sb = work.tile([P, TILES, WIDTH], F32, name="out_sb")
            for j in range(TILES):
                o_ps = psum.tile([P, WIDTH], F32, name="o_ps", tag="bank")
                nc.tensor.matmul_mx(
                    out=o_ps[:],
                    lhsT=h_codes[:, j * P : (j + 1) * P].bitcast(FP8X4),
                    lhsT_scale=h_scales[:, j * P : (j + 1) * P],
                    rhs=wp_codes[:].bitcast(FP8X4),
                    rhs_scale=wp_scales[:],
                    start=True,
                    stop=True,
                )
                if j < VECTOR_BANKS:
                    nc.vector.tensor_copy(out=out_sb[:, j, :], in_=o_ps[:])
                else:
                    nc.scalar.copy(out=out_sb[:, j, :], in_=o_ps[:])
                nc.sync.dma_start(out=out_blocks[n][:, j, :], in_=out_sb[:, j, :])

        def prepare_weights():
            wg_grouped = consts.tile([P, WIDTH, PACK], BF16, name="wg_grouped", align_bytes=64)
            nc.vector.tensor_copy(out=wg_grouped[:], in_=wg_raw[:].rearrange("p t c -> p c t"))
            wp_grouped = consts.tile([P, WIDTH, PACK], BF16, name="wp_grouped", align_bytes=64)
            nc.vector.tensor_copy(out=wp_grouped[:], in_=wp_raw[:].rearrange("p t c -> p c t"))
            live["wg_mx"] = quantise(wg_grouped[:].rearrange("p c t -> p (c t)"), consts, "wg")
            live["wp_mx"] = quantise(wp_grouped[:].rearrange("p c t -> p (c t)"), consts, "wp")
            affine_ps = psum.tile([P, P], BF16, name="affine_ps", tag="bank")
            nc.tensor.transpose(affine_ps[:], affine_rows[:], ident_bf16[:])
            nc.vector.tensor_copy(out=gain_bias[:], in_=affine_ps[:, 0 : 2 * HEADS])

        load(0)
        wg_raw = consts.tile([P, PACK, WIDTH], BF16, name="wg_raw")
        nc.sync.dma_start(
            out=wg_raw[:].rearrange("p (u e) c -> p u e c", u=2), in_=w_g.rearrange("(u p e) c -> p u e c", u=2, e=2)
        )
        affine_rows = consts.tile([P, P], BF16, name="affine_rows")
        nc.vector.memset(affine_rows[:], 0.0)
        nc.sync.dma_start(out=affine_rows[0:HEADS, :], in_=gn_weight.rearrange("(t p) -> t p", t=HEADS))
        nc.sync.dma_start(out=affine_rows[HEADS : 2 * HEADS, :], in_=gn_bias.rearrange("(t p) -> t p", t=HEADS))
        wp_raw = consts.tile([P, PACK, WIDTH], BF16, name="wp_raw")
        nc.sync.dma_start(out=wp_raw[:], in_=w_proj.rearrange("(t p) n -> p t n", t=PACK))
        for n in range(1, LOAD_AHEAD):
            load(n)

        ident_f32 = consts.tile([P, P], F32, name="ident_f32")
        make_identity(nc, ident_f32[:])
        ident_bf16 = consts.tile([P, P], BF16, name="ident_bf16")
        make_identity(nc, ident_bf16[:])
        minus_half = consts.tile([P, TILES * HEADS], F32, name="minus_half")
        nc.vector.memset(minus_half[:], -0.5)
        gain_bias = consts.tile([P, 2 * HEADS], F32, name="gain_bias")
        table_warmer = consts.tile([P, 1], F32, name="table_warmer")
        nc.scalar.activation(out=table_warmer[:], in_=minus_half[:, 0:1], func=ACT.Silu)

        def run(stage, n):
            if 0 <= n < BLOCKS:
                stage(n)

        for step in range(BLOCKS + LAST_STAGE):
            run(quantise_tokens, step - 1)
            if step == WEIGHTS_STEP:
                prepare_weights()
            run(multiply, step - 3)
            run(statistics, step)
            run(quantise_hidden, step - 3)
            run(centre_and_scale, step - 1)
            run(project, step - 4)
            run(gate, step - 2)
            run(affine, step - 2)
            run(transpose_tokens, step)
            run(load, step + LOAD_AHEAD)
